import numpy as np
import ml_dtypes


def mxq(x, axis, fmt="e4m3"):
    dtype, down = {"e4m3": (ml_dtypes.float8_e4m3fn, 7), "e5m2": (ml_dtypes.float8_e5m2, 14)}[fmt]
    v = np.moveaxis(np.asarray(x, np.float32).astype(ml_dtypes.bfloat16).astype(np.float64), axis, -1)
    blocks = v.reshape(v.shape[:-1] + (-1, 32))
    amax = np.abs(blocks).max(-1, keepdims=True)
    byte = np.maximum(np.where(amax > 0, np.frexp(amax)[1] - 1 + 127, 0) - down, 1)
    scale = np.exp2(byte - 127.0)
    codes = (blocks / scale).astype(np.float32).astype(dtype).astype(np.float64)
    return np.moveaxis((codes * scale).reshape(v.shape), -1, axis)


WIDE = False


def mx_kscale(k):
    if not WIDE:
        return np.ones(k)
    levels = np.array([10, -10, 5, -5, 0])
    a = np.random.permutation(np.resize(levels, k // 512 * 4)).reshape(k // 512, 4)
    idx = np.arange(k)
    return np.exp2(a[idx // 512, idx % 128 // 32])


BF16 = ml_dtypes.bfloat16


def bf(x):
    return np.asarray(x, np.float32).astype(BF16)


def f64(x):
    return np.asarray(x).astype(np.float64)


B, IN, OUT, CHEBY_ORDER = 1024, 512, 512, 10


def silu(v):
    return v / (1.0 + np.exp(-v))


def chebyshev_bases(x, order):
    t0 = np.ones_like(x)
    if order == 1:
        return t0[None]
    ts = [t0, x]
    for _ in range(2, order):
        ts.append(2.0 * x * ts[-1] - ts[-2])
    return np.stack(ts)


def setup_inputs():
    u = np.minimum(mx_kscale(IN), 1.0) ** 2
    return {"x": bf(np.random.random_sample((B, IN)) * u),
            "base_weight": bf(np.random.standard_normal((OUT, IN)) * 0.05 / u),
            "cheby_weight": bf(np.random.standard_normal((OUT, IN, CHEBY_ORDER)) * 0.05)}


def reference(x, base_weight, cheby_weight):
    x = f64(x)
    base_weight = f64(base_weight)
    cheby_weight = f64(cheby_weight)
    b, n_in = x.shape
    n_out, _, o = cheby_weight.shape
    base_out = mxq(silu(x), 1, "e4m3") @ mxq(base_weight, 1, "e4m3").T
    bases = chebyshev_bases(x, o)
    flat = bases.reshape(b, o * n_in)
    w = cheby_weight.reshape(n_out, n_in * o)
    spline_out = (mxq(flat, 1, "e4m3") @ mxq(w, 1, "e4m3").T) / o
    return base_out + spline_out

@@ -1,0 +1,430 @@
+from contextlib import ExitStack
+
+import concourse.mybir as mybir
+from concourse.masks import make_identity
+
+F32 = mybir.dt.float32
+BF16 = mybir.dt.bfloat16
+U32 = mybir.dt.uint32
+U8 = mybir.dt.uint8
+FP8X4 = mybir.dt.float8_e4m3fn_x4
+ALU = mybir.AluOpType
+ACTF = mybir.ActivationFunctionType
+
+P = 128
+B = 1024
+IN = 512
+OUT = 512
+ORDER = 10
+FLOPS = 2 * B * OUT * (IN + IN * ORDER)
+
+ND = 10
+EP = 104
+XROWS = 120
+CA = (0, 48)
+CB = (48, EP)
+MANUAL = True
+
+
+def count_e(d):
+    return 103 if d < 4 else 102
+
+
+def runs(n, da, db, ea, eb):
+    found = []
+    d0 = da
+    while d0 < db:
+        q = (4 * n + d0) // 10
+        d1 = d0
+        while d1 < db and (4 * n + d1) // 10 == q and count_e(d1) == count_e(d0):
+            d1 += 1
+        start = 102 * n + q
+        lo = ea
+        hi = min(eb, count_e(d0))
+        while lo < hi:
+            j = (start + lo) // P
+            end = min(hi, P * (j + 1) - start)
+            found.append((d0, d1, lo, end, j, (4 * n + d0) % 10, (start + lo) % P, lo == 0, end == count_e(d0)))
+            lo = end
+        d0 = d1
+    return found
+
+
+def tile_kantlinear_kernel(tc, x, base_weight, cheby_weight, out):
+    nc = tc.nc
+    with ExitStack() as ctx:
+        if MANUAL:
+            ctx.enter_context(tc.manual_schedule())
+        keep = ctx.enter_context(tc.tile_pool(name="keep", bufs=1))
+        wraw = ctx.enter_context(tc.tile_pool(name="wraw", bufs=3))
+        wgrp = ctx.enter_context(tc.tile_pool(name="wgrp", bufs=3))
+        gpool = ctx.enter_context(tc.tile_pool(name="gpool", bufs=3))
+        cpool = ctx.enter_context(tc.tile_pool(name="cpool", bufs=4))
+        opool = ctx.enter_context(tc.tile_pool(name="opool", bufs=3))
+        psum = ctx.enter_context(tc.psum_pool(name="psum", bufs=1))
+
+        def bank(i, name):
+            return psum.tile([P, 2, 256], F32, tag="bank%d" % i, name=name)
+
+        warm = keep.tile([P, 1], F32, name="warm")
+        nc.vector.memset(warm[:], 0.0)
+        nc.scalar.activation(out=warm[:], in_=warm[:], func=ACTF.Silu)
+
+        xs = keep.tile([P, 9, IN], BF16, name="xs")
+        for t in range(9):
+            r0 = XROWS * t if t < 8 else B - P
+            nc.sync.dma_start(out=xs[:, t, :], in_=x[r0 : r0 + P, :])
+        wv = cheby_weight.rearrange("o i k -> o (i k)").rearrange("(t p) k -> p t k", p=P)
+        bv = base_weight.rearrange("(t p) k -> p t k", p=P)
+        raws = {}
+
+        def w_load(cc):
+            if cc < 5:
+                raws[cc] = wraw.tile([P, 4, 1024], BF16, tag="wr", name="wr%d" % cc)
+                nc.sync.dma_start(out=raws[cc][:], in_=wv[:, :, 1024 * cc : 1024 * cc + 1024])
+            else:
+                raws[cc] = wraw.tile([P, 4, IN], BF16, tag="wr", name="wrb")
+                nc.sync.dma_start(out=raws[cc][:], in_=bv)
+
+        ident = keep.tile([P, P], F32, name="ident")
+        make_identity(nc, ident[:])
+
+        xg = keep.tile([P, ND, EP, 4], BF16, name="xg", align_bytes=64)
+        nc.vector.memset(xg[:, :, 100:EP, :], 0.0)
+        xgw = (
+            xg[:]
+            .rearrange("p d e t -> p (d e t)")
+            .bitcast(F32)
+            .rearrange("p (d e u) -> p d e u", d=ND, e=EP, u=2)
+        )
+
+        gt = {}
+
+        def g_tile(j):
+            if j not in gt:
+                gt[j] = gpool.tile([P, ORDER, P, 4], BF16, tag="G", name="G%d" % j, align_bytes=64)
+            return gt[j]
+
+        for d0, d1, e0, e1, j, c0, m0, first, last in runs(0, 0, ND, 0, EP):
+            nc.vector.memset(g_tile(j)[:, c0 : c0 + d1 - d0, m0 : m0 + e1 - e0, :], 1.0)
+
+        xp = [bank(k, "xp%d" % k) for k in range(5)]
+
+        def x_transpose(t):
+            words = xs[:, t, :].bitcast(F32)
+            for u in range(2):
+                nc.tensor.transpose(
+                    xp[t // 2][:, u, P * (t % 2) : P * (t % 2) + P], words[:, P * u : P * u + P], ident[:]
+                )
+
+        def copy_out(on_act, dst, src):
+            if on_act:
+                nc.scalar.copy(out=dst, in_=src)
+            else:
+                nc.vector.tensor_copy(out=dst, in_=src)
+
+        def x_copy(t, on_act):
+            col = P * (t % 2)
+            if t < 8:
+                copy_out(
+                    on_act,
+                    xgw[:, :, 12 * t : 12 * t + 12, :],
+                    xp[t // 2][:, :, col : col + XROWS].rearrange("p u (e d) -> p d e u", e=12, d=ND),
+                )
+            else:
+                copy_out(
+                    on_act,
+                    xgw[:, :, 96:102, :],
+                    xp[4][:, :, 64:124].rearrange("p u (e d) -> p d e u", e=6, d=ND),
+                )
+                copy_out(on_act, xgw[:, 0:4, 102, :], xp[4][:, :, 124:128].rearrange("p u d -> p d u"))
+
+        wcodes = keep.tile([P, ORDER + 1, OUT], U32, name="wcodes", align_bytes=64)
+        wscales = keep.tile([P, ORDER + 1, OUT], U8, name="wscales", align_bytes=64)
+        state = {"wbank": 0}
+        grouped = {}
+
+        def w_quant(g):
+            nc.vector.quantize_mx(
+                out=wcodes[:, g, :].bitcast(FP8X4),
+                scales=wscales[:, g, :],
+                in_=grouped[g][:].rearrange("p o t -> p (o t)"),
+            )
+
+        def w_pass(g, act_halves=(True, True)):
+            raw = raws[g // 2]
+            word0 = 256 * (g % 2)
+            grouped[g] = wgrp.tile([P, OUT, 4], BF16, tag="wg", name="wg%d" % g, align_bytes=64)
+            gw = grouped[g][:].rearrange("p o t -> p (o t)").bitcast(F32).rearrange("p (o u) -> p o u", u=2)
+            for half in range(2):
+                wt = bank(5 + state["wbank"] % 3, "wt%d_%d" % (g, half))
+                state["wbank"] += 1
+                for u in range(2):
+                    for oo in range(2):
+                        words = raw[:, 2 * half + oo, :].bitcast(F32)
+                        nc.tensor.transpose(
+                            wt[:, u, P * oo : P * oo + P],
+                            words[:, word0 + P * u : word0 + P * u + P],
+                            ident[:],
+                        )
+                copy_out(
+                    act_halves[half], gw[:, 256 * half : 256 * half + 256, :], wt[:].rearrange("p u o -> p o u")
+                )
+
+        sg = keep.tile([P, B, 4], BF16, name="sg", align_bytes=64)
+        scodes = keep.tile([P, B], U32, name="scodes", align_bytes=64)
+        sscales = keep.tile([P, B], U8, name="sscales", align_bytes=64)
+
+        def silu(t):
+            halves = (
+                xp[t // 2][:]
+                .rearrange("p u c -> p (u c)")
+                .bitcast(BF16)
+                .rearrange("p (u c e) -> p u c e", u=2, c=256, e=2)
+            )
+            c0 = P * (t % 2) if t < 8 else 64
+            n_col = XROWS if t < 8 else 64
+            nc.scalar.activation(
+                out=sg[:, XROWS * t : XROWS * t + n_col, :].rearrange("p c (u e) -> p c u e", u=2),
+                in_=halves[:, :, c0 : c0 + n_col, :].rearrange("p u c e -> p c u e"),
+                func=ACTF.Silu,
+            )
+
+        def silu_quant():
+            nc.vector.quantize_mx(
+                out=scodes[:].bitcast(FP8X4), scales=sscales[:], in_=sg[:].rearrange("p c t -> p (c t)")
+            )
+
+        codes = {}
+        sums = {}
+
+        def quant(j, c0=0, c1=ORDER):
+            if j not in codes:
+                codes[j] = (
+                    cpool.tile([P, ORDER * P], U32, tag="fc", name="fc%d" % j, align_bytes=64),
+                    cpool.tile([P, ORDER * P], U8, tag="fs", name="fs%d" % j, align_bytes=64),
+                )
+            fc, fs = codes[j]
+            flat = gt[j][:].rearrange("p c m t -> p (c m t)")
+            while c0 < c1:
+                width = 8 if c1 - c0 >= 8 else 4 if c1 - c0 >= 4 else 2 if c1 - c0 >= 2 else 1
+                nc.vector.quantize_mx(
+                    out=fc[:, P * c0 : P * (c0 + width)].bitcast(FP8X4),
+                    scales=fs[:, P * c0 : P * (c0 + width)],
+                    in_=flat[:, 4 * P * c0 : 4 * P * (c0 + width)],
+                )
+                c0 += width
+
+        def base(j):
+            accb = psum.tile([P, OUT], F32, tag="bank%d" % (4 + j % 4), name="accb%d" % j)
+            nc.tensor.matmul_mx(
+                out=accb[:],
+                lhsT=scodes[:, P * j : P * j + P].bitcast(FP8X4),
+                lhsT_scale=sscales[:, P * j : P * j + P],
+                rhs=wcodes[:, ORDER, :].bitcast(FP8X4),
+                rhs_scale=wscales[:, ORDER, :],
+                start=True,
+                stop=True,
+            )
+            bsb = opool.tile([P, OUT], F32, tag="bsb", name="bsb%d" % j)
+            nc.scalar.copy(out=bsb[:], in_=accb[:])
+            sums[j] = [None, bsb]
+
+        def spline(j, c0=0, c1=ORDER):
+            fc, fs = codes[j]
+            if c0 == 0:
+                sums[j][0] = psum.tile([P, OUT], F32, tag="bank%d" % (j % 4), name="accs%d" % j)
+            for c in range(c0, c1):
+                nc.tensor.matmul_mx(
+                    out=sums[j][0][:],
+                    lhsT=fc[:, P * c : P * c + P].bitcast(FP8X4),
+                    lhsT_scale=fs[:, P * c : P * c + P],
+                    rhs=wcodes[:, c, :].bitcast(FP8X4),
+                    rhs_scale=wscales[:, c, :],
+                    start=(c == 0),
+                    stop=(c == ORDER - 1),
+                )
+
+        def store(j):
+            accs, bsb = sums[j]
+            osb = opool.tile([P, OUT], F32, tag="osb", name="osb%d" % j)
+            nc.vector.scalar_tensor_tensor(
+                out=osb[:], in0=accs[:], scalar=0.1, in1=bsb[:], op0=ALU.mult, op1=ALU.add
+            )
+            nc.sync.dma_start(out=out[P * j : P * j + P, :], in_=osb[:])
+
+        def temp(tag):
+            return keep.tile([P, ND, EP, 4], F32, tag=tag, name=tag)
+
+        def square(dst, src, scale, bias, chunk):
+            e0, e1 = chunk
+            nc.scalar.activation(
+                out=dst[:, :, e0:e1, :], in_=src[:, :, e0:e1, :], func=ACTF.Square, scale=scale, bias=bias
+            )
+
+        def product(dst, a, shift, b, chunk):
+            e0, e1 = chunk
+            nc.vector.scalar_tensor_tensor(
+                out=dst[:, :, e0:e1, :],
+                in0=a[:, :, e0:e1, :],
+                scalar=shift,
+                in1=b[:, :, e0:e1, :],
+                op0=ALU.subtract,
+                op1=ALU.mult,
+            )
+
+        def to_g(n, emit, chunk, emit_act=None, d_range=(0, ND)):
+            for d0, d1, e0, e1, j, c0, m0, first, last in runs(n, d_range[0], d_range[1], chunk[0], chunk[1]):
+                g = g_tile(j)
+                parts = [(e0, e1, False)]
+                if emit_act is not None:
+                    lo = e0 + (-m0) % 4 if first else e0
+                    hi = e1 - (m0 + e1 - e0) % 4 if last else e1
+                    if lo < hi:
+                        parts = [(lo, hi, True), (e0, lo, False), (hi, e1, False)]
+                for a, b, on_act in parts:
+                    if a == b:
+                        continue
+                    dst = g[:, c0 : c0 + d1 - d0, m0 + a - e0 : m0 + b - e0, :]
+                    (emit_act if on_act else emit)(dst, (slice(None), slice(d0, d1), slice(a, b), slice(None)))
+
+        def affine(src, scale, bias):
+            def on_vector(dst, where):
+                nc.vector.tensor_scalar(
+                    out=dst, in0=src[where], scalar1=scale, scalar2=bias, op0=ALU.mult, op1=ALU.add
+                )
+
+            return on_vector
+
+        def affine_act(src, scale, bias):
+            def on_scalar(dst, where):
+                nc.scalar.activation(out=dst, in_=src[where], func=ACTF.Identity, scale=scale, bias=bias)
+
+            return on_scalar
+
+        def cast(n, src, scale, bias, chunk, on_act=False):
+            to_g(n, affine(src, scale, bias), chunk, affine_act(src, scale, bias) if on_act else None)
+
+        def shifted_product(a, shift, b):
+            def on_vector(dst, where):
+                nc.vector.scalar_tensor_tensor(
+                    out=dst, in0=a[where], scalar=shift, in1=b[where], op0=ALU.subtract, op1=ALU.mult
+                )
+
+            return on_vector
+
+        def scaled_minus(a, scale, b):
+            def on_vector(dst, where):
+                nc.vector.scalar_tensor_tensor(
+                    out=dst, in0=a[where], scalar=scale, in1=b[where], op0=ALU.mult, op1=ALU.subtract
+                )
+
+            return on_vector
+
+        def plain_copy(src):
+            def on_vector(dst, where):
+                nc.vector.tensor_copy(out=dst, in_=src[where])
+
+            return on_vector
+
+        for cc in range(3):
+            w_load(cc)
+        for t in range(9):
+            x_transpose(t)
+        x2 = temp("ta")
+        h3 = temp("tb")
+        y4 = temp("tc")
+        y5 = temp("td")
+        for t in range(4):
+            x_copy(t, True)
+        square(x2, xg, 1.0, 0.0, CA)
+        for t in range(4, 9):
+            x_copy(t, True)
+        square(x2, xg, 1.0, 0.0, CB)
+        to_g(1, plain_copy(xg), CA)
+        quant(0)
+        cast(2, x2, 2.0, -1.0, CA)
+        to_g(1, plain_copy(xg), CB)
+        product(h3, x2, 0.75, xg, CA)
+        for g in range(4):
+            w_pass(g)
+        w_load(3)
+        w_load(4)
+        cast(2, x2, 2.0, -1.0, CB)
+        product(h3, x2, 0.75, xg, CB)
+        square(y4, x2, 2.0, -1.0, CA)
+        square(y4, x2, 2.0, -1.0, CB)
+        for g in range(4):
+            w_quant(g)
+        quant(1)
+        cast(3, h3, 4.0, 0.0, CA)
+        cast(3, h3, 4.0, 0.0, CB)
+        for g in range(4, 8):
+            w_pass(g)
+        w_load(5)
+        square(y5, x2, 4.0, -2.5, CA)
+        square(y5, x2, 4.0, -2.5, CB)
+        quant(2)
+        cast(4, y4, 2.0, -1.0, CA)
+        cast(4, y4, 2.0, -1.0, CB)
+        for g in range(4, 8):
+            w_quant(g)
+        for g in range(8, 11):
+            w_pass(g)
+        for t in range(9):
+            silu(t)
+        y6 = temp("ta")
+        square(y6, h3, 16.0, 0.0, CA)
+        square(y6, h3, 16.0, 0.0, CB)
+        to_g(5, shifted_product(y5, 1.25, xg), CA)
+        quant(3)
+        to_g(5, shifted_product(y5, 1.25, xg), CB)
+        for g in range(8, 11):
+            w_quant(g)
+        silu_quant()
+        t7 = temp("td")
+        product(t7, y4, 0.5, h3, CA)
+        for j in range(2):
+            base(j)
+            spline(j)
+        product(t7, y4, 0.5, h3, CB)
+        square(y4, y4, 2.0, -1.0, CA)
+        square(y4, y4, 2.0, -1.0, CB)
+        cast(6, y6, 0.125, -1.0, CA)
+        cast(6, y6, 0.125, -1.0, CB)
+        store(0)
+        store(1)
+        for j in range(2, 4):
+            base(j)
+            spline(j)
+        quant(4)
+        to_g(7, scaled_minus(t7, 16.0, xg), CA)
+        to_g(7, scaled_minus(t7, 16.0, xg), CB)
+        store(2)
+        store(3)
+        base(4)
+        spline(4)
+        quant(5)
+        cast(8, y4, 2.0, -1.0, CA)
+        cast(8, y4, 2.0, -1.0, CB)
+        base(5)
+        spline(5)
+        whole = (0, EP)
+        to_g(9, shifted_product(y6, 12.0, h3), whole, d_range=(4, 8))
+        quant(6)
+        store(4)
+        base(6)
+        spline(6)
+        base(7)
+        to_g(9, shifted_product(y6, 12.0, h3), whole, d_range=(8, 10))
+        to_g(9, shifted_product(y6, 12.0, h3), whole, d_range=(0, 2))
+        quant(7, 0, 4)
+        spline(7, 0, 4)
+        to_g(9, shifted_product(y6, 12.0, h3), whole, d_range=(2, 4))
+        quant(7, 4, 8)
+        spline(7, 4, 8)
+        store(5)
+        quant(7, 8, 10)
+        spline(7, 8, 10)
+        store(6)
+        store(7)

@@ -23,6 +23,7 @@ EP = 104
 XROWS = 120
 CA = (0, 48)
 CB = (48, EP)
+CW = (0, EP)
 MANUAL = True
 
 
@@ -228,12 +229,15 @@ def tile_kantlinear_kernel(tc, x, base_weight, cheby_weight, out):
             )
             bsb = opool.tile([P, OUT], F32, tag="bsb", name="bsb%d" % j)
             nc.scalar.copy(out=bsb[:], in_=accb[:])
-            sums[j] = [None, bsb]
+            sums[j] = [sums[j][0] if j in sums else None, bsb]
 
         def spline(j, c0=0, c1=ORDER):
             fc, fs = codes[j]
             if c0 == 0:
-                sums[j][0] = psum.tile([P, OUT], F32, tag="bank%d" % (j % 4), name="accs%d" % j)
+                sums[j] = [
+                    psum.tile([P, OUT], F32, tag="bank%d" % (j % 4), name="accs%d" % j),
+                    sums[j][1] if j in sums else None,
+                ]
             for c in range(c0, c1):
                 nc.tensor.matmul_mx(
                     out=sums[j][0][:],
@@ -253,22 +257,31 @@ def tile_kantlinear_kernel(tc, x, base_weight, cheby_weight, out):
             )
             nc.sync.dma_start(out=out[P * j : P * j + P, :], in_=osb[:])
 
-        def temp(tag):
-            return keep.tile([P, ND, EP, 4], F32, tag=tag, name=tag)
+        tags = {"x2": "ta", "y6": "ta", "h3": "tb", "y4": "tc", "y5": "td", "t7": "td"}
+        temps = {"x": xg}
+
+        def tmp(name):
+            if name not in temps:
+                temps[name] = keep.tile([P, ND, EP, 4], F32, tag=tags[name], name=name)
+            return temps[name]
 
         def square(dst, src, scale, bias, chunk):
             e0, e1 = chunk
             nc.scalar.activation(
-                out=dst[:, :, e0:e1, :], in_=src[:, :, e0:e1, :], func=ACTF.Square, scale=scale, bias=bias
+                out=tmp(dst)[:, :, e0:e1, :],
+                in_=tmp(src)[:, :, e0:e1, :],
+                func=ACTF.Square,
+                scale=scale,
+                bias=bias,
             )
 
         def product(dst, a, shift, b, chunk):
             e0, e1 = chunk
             nc.vector.scalar_tensor_tensor(
-                out=dst[:, :, e0:e1, :],
-                in0=a[:, :, e0:e1, :],
+                out=tmp(dst)[:, :, e0:e1, :],
+                in0=tmp(a)[:, :, e0:e1, :],
                 scalar=shift,
-                in1=b[:, :, e0:e1, :],
+                in1=tmp(b)[:, :, e0:e1, :],
                 op0=ALU.subtract,
                 op1=ALU.mult,
             )
@@ -291,14 +304,14 @@ def tile_kantlinear_kernel(tc, x, base_weight, cheby_weight, out):
         def affine(src, scale, bias):
             def on_vector(dst, where):
                 nc.vector.tensor_scalar(
-                    out=dst, in0=src[where], scalar1=scale, scalar2=bias, op0=ALU.mult, op1=ALU.add
+                    out=dst, in0=tmp(src)[where], scalar1=scale, scalar2=bias, op0=ALU.mult, op1=ALU.add
                 )
 
             return on_vector
 
         def affine_act(src, scale, bias):
             def on_scalar(dst, where):
-                nc.scalar.activation(out=dst, in_=src[where], func=ACTF.Identity, scale=scale, bias=bias)
+                nc.scalar.activation(out=dst, in_=tmp(src)[where], func=ACTF.Identity, scale=scale, bias=bias)
 
             return on_scalar
 
@@ -308,7 +321,7 @@ def tile_kantlinear_kernel(tc, x, base_weight, cheby_weight, out):
         def shifted_product(a, shift, b):
             def on_vector(dst, where):
                 nc.vector.scalar_tensor_tensor(
-                    out=dst, in0=a[where], scalar=shift, in1=b[where], op0=ALU.subtract, op1=ALU.mult
+                    out=dst, in0=tmp(a)[where], scalar=shift, in1=tmp(b)[where], op0=ALU.subtract, op1=ALU.mult
                 )
 
             return on_vector
@@ -316,111 +329,144 @@ def tile_kantlinear_kernel(tc, x, base_weight, cheby_weight, out):
         def scaled_minus(a, scale, b):
             def on_vector(dst, where):
                 nc.vector.scalar_tensor_tensor(
-                    out=dst, in0=a[where], scalar=scale, in1=b[where], op0=ALU.mult, op1=ALU.subtract
+                    out=dst, in0=tmp(a)[where], scalar=scale, in1=tmp(b)[where], op0=ALU.mult, op1=ALU.subtract
                 )
 
             return on_vector
 
         def plain_copy(src):
             def on_vector(dst, where):
-                nc.vector.tensor_copy(out=dst, in_=src[where])
+                nc.vector.tensor_copy(out=dst, in_=tmp(src)[where])
 
             return on_vector
 
-        for cc in range(3):
-            w_load(cc)
-        for t in range(9):
-            x_transpose(t)
-        x2 = temp("ta")
-        h3 = temp("tb")
-        y4 = temp("tc")
-        y5 = temp("td")
-        for t in range(4):
-            x_copy(t, True)
-        square(x2, xg, 1.0, 0.0, CA)
-        for t in range(4, 9):
-            x_copy(t, True)
-        square(x2, xg, 1.0, 0.0, CB)
-        to_g(1, plain_copy(xg), CA)
+        w_load(0)
+        w_load(1)
+        w_load(2)
+        x_transpose(0)
+        x_transpose(1)
+        x_transpose(2)
+        x_transpose(3)
+        x_transpose(4)
+        x_transpose(5)
+        x_transpose(6)
+        x_transpose(7)
+        x_transpose(8)
+        x_copy(0, True)
+        x_copy(1, True)
+        x_copy(2, True)
+        x_copy(3, True)
+        x_copy(5, True)
+        square("x2", "x", 1.0, 0.0, CA)
+        x_copy(4, True)
+        x_copy(6, True)
+        x_copy(7, True)
+        x_copy(8, True)
+        square("x2", "x", 1.0, 0.0, CB)
+        to_g(1, plain_copy("x"), CA)
         quant(0)
-        cast(2, x2, 2.0, -1.0, CA)
-        to_g(1, plain_copy(xg), CB)
-        product(h3, x2, 0.75, xg, CA)
-        for g in range(4):
-            w_pass(g)
+        cast(2, "x2", 2.0, -1.0, CA)
+        to_g(1, plain_copy("x"), CB)
+        product("h3", "x2", 0.75, "x", CA)
+        w_pass(0)
+        w_pass(1)
+        w_pass(2)
+        w_pass(3)
         w_load(3)
         w_load(4)
-        cast(2, x2, 2.0, -1.0, CB)
-        product(h3, x2, 0.75, xg, CB)
-        square(y4, x2, 2.0, -1.0, CA)
-        square(y4, x2, 2.0, -1.0, CB)
-        for g in range(4):
-            w_quant(g)
+        cast(2, "x2", 2.0, -1.0, CB)
+        product("h3", "x2", 0.75, "x", CB)
+        square("y4", "x2", 2.0, -1.0, CA)
+        square("y4", "x2", 2.0, -1.0, CB)
+        w_quant(0)
+        w_quant(1)
+        w_quant(2)
+        w_quant(3)
         quant(1)
-        cast(3, h3, 4.0, 0.0, CA)
-        cast(3, h3, 4.0, 0.0, CB)
-        for g in range(4, 8):
-            w_pass(g)
-        w_load(5)
-        square(y5, x2, 4.0, -2.5, CA)
-        square(y5, x2, 4.0, -2.5, CB)
+        cast(3, "h3", 4.0, 0.0, CA)
+        cast(3, "h3", 4.0, 0.0, CB)
+        w_pass(4)
+        w_pass(5)
+        w_pass(6)
+        square("y5", "x2", 4.0, -2.5, CB)
         quant(2)
-        cast(4, y4, 2.0, -1.0, CA)
-        cast(4, y4, 2.0, -1.0, CB)
-        for g in range(4, 8):
-            w_quant(g)
-        for g in range(8, 11):
-            w_pass(g)
-        for t in range(9):
-            silu(t)
-        y6 = temp("ta")
-        square(y6, h3, 16.0, 0.0, CA)
-        square(y6, h3, 16.0, 0.0, CB)
-        to_g(5, shifted_product(y5, 1.25, xg), CA)
+        w_pass(7)
+        w_load(5)
+        square("y5", "x2", 4.0, -2.5, CA)
+        cast(4, "y4", 2.0, -1.0, CA)
+        cast(4, "y4", 2.0, -1.0, CB)
+        w_quant(4)
+        w_quant(5)
+        w_quant(6)
+        w_quant(7)
+        w_pass(8)
+        silu(1)
+        silu(3)
+        silu(4)
+        silu(5)
+        w_pass(9)
+        silu(0)
+        silu(2)
+        silu(6)
+        w_pass(10)
+        silu(7)
+        silu(8)
+        square("y6", "h3", 16.0, 0.0, CA)
+        square("y6", "h3", 16.0, 0.0, CB)
+        to_g(5, shifted_product("y5", 1.25, "x"), CA)
         quant(3)
-        to_g(5, shifted_product(y5, 1.25, xg), CB)
-        for g in range(8, 11):
-            w_quant(g)
+        to_g(5, shifted_product("y5", 1.25, "x"), CB)
+        w_quant(8)
+        w_quant(9)
+        spline(2, 0, 4)
+        w_quant(10)
+        spline(0, 0, 4)
         silu_quant()
-        t7 = temp("td")
-        product(t7, y4, 0.5, h3, CA)
-        for j in range(2):
-            base(j)
-            spline(j)
-        product(t7, y4, 0.5, h3, CB)
-        square(y4, y4, 2.0, -1.0, CA)
-        square(y4, y4, 2.0, -1.0, CB)
-        cast(6, y6, 0.125, -1.0, CA)
-        cast(6, y6, 0.125, -1.0, CB)
+        spline(0, 4, 8)
+        product("t7", "y4", 0.5, "h3", CA)
+        base(1)
+        base(0)
+        spline(1, 0, 4)
+        spline(1, 4, 8)
+        spline(0, 8, 10)
+        spline(1, 8, 10)
+        product("t7", "y4", 0.5, "h3", CB)
+        cast(6, "y6", 0.125, -1.0, CA, True)
         store(0)
+        square("y4", "y4", 2.0, -1.0, CA)
+        square("y4", "y4", 2.0, -1.0, CB)
         store(1)
-        for j in range(2, 4):
-            base(j)
-            spline(j)
+        spline(2, 4, 8)
+        base(2)
+        base(3)
+        spline(3, 0, 4)
+        spline(2, 8, 10)
+        spline(3, 4, 8)
+        cast(6, "y6", 0.125, -1.0, CB, True)
+        spline(3, 8, 10)
         quant(4)
-        to_g(7, scaled_minus(t7, 16.0, xg), CA)
-        to_g(7, scaled_minus(t7, 16.0, xg), CB)
+        to_g(7, scaled_minus("t7", 16.0, "x"), CA)
+        to_g(7, scaled_minus("t7", 16.0, "x"), CB)
         store(2)
         store(3)
         base(4)
         spline(4)
         quant(5)
-        cast(8, y4, 2.0, -1.0, CA)
-        cast(8, y4, 2.0, -1.0, CB)
+        cast(8, "y4", 2.0, -1.0, CA, True)
+        cast(8, "y4", 2.0, -1.0, CB, True)
         base(5)
-        spline(5)
-        whole = (0, EP)
-        to_g(9, shifted_product(y6, 12.0, h3), whole, d_range=(4, 8))
-        quant(6)
         store(4)
+        spline(5)
+        to_g(9, shifted_product("y6", 12.0, "h3"), CW, d_range=(4, 8))
+        quant(6)
         base(6)
-        spline(6)
         base(7)
-        to_g(9, shifted_product(y6, 12.0, h3), whole, d_range=(8, 10))
-        to_g(9, shifted_product(y6, 12.0, h3), whole, d_range=(0, 2))
+        to_g(9, shifted_product("y6", 12.0, "h3"), CW, d_range=(8, 10))
+        to_g(9, shifted_product("y6", 12.0, "h3"), CW, d_range=(0, 2))
+        spline(6)
         quant(7, 0, 4)
         spline(7, 0, 4)
-        to_g(9, shifted_product(y6, 12.0, h3), whole, d_range=(2, 4))
+        to_g(9, shifted_product("y6", 12.0, "h3"), CW, d_range=(2, 4))
         quant(7, 4, 8)
         spline(7, 4, 8)
         store(5)

@@ -347,7 +347,6 @@ def tile_kantlinear_kernel(tc, x, base_weight, cheby_weight, out):
         x_transpose(1)
         x_transpose(2)
         x_transpose(3)
-        x_transpose(4)
         x_transpose(5)
         x_transpose(6)
         x_transpose(7)
@@ -356,7 +355,8 @@ def tile_kantlinear_kernel(tc, x, base_weight, cheby_weight, out):
         x_copy(1, True)
         x_copy(2, True)
         x_copy(3, True)
-        x_copy(5, True)
+        x_copy(5, False)
+        x_transpose(4)
         square("x2", "x", 1.0, 0.0, CA)
         x_copy(4, True)
         x_copy(6, True)
@@ -366,45 +366,45 @@ def tile_kantlinear_kernel(tc, x, base_weight, cheby_weight, out):
         to_g(1, plain_copy("x"), CA)
         quant(0)
         cast(2, "x2", 2.0, -1.0, CA)
-        to_g(1, plain_copy("x"), CB)
         product("h3", "x2", 0.75, "x", CA)
         w_pass(0)
+        to_g(1, plain_copy("x"), CB)
         w_pass(1)
         w_pass(2)
-        w_pass(3)
-        w_load(3)
-        w_load(4)
-        cast(2, "x2", 2.0, -1.0, CB)
         product("h3", "x2", 0.75, "x", CB)
         square("y4", "x2", 2.0, -1.0, CA)
-        square("y4", "x2", 2.0, -1.0, CB)
         w_quant(0)
         w_quant(1)
         w_quant(2)
-        w_quant(3)
-        quant(1)
-        cast(3, "h3", 4.0, 0.0, CA)
-        cast(3, "h3", 4.0, 0.0, CB)
+        w_load(4)
+        cast(2, "x2", 2.0, -1.0, CB)
+        w_pass(3)
+        w_load(3)
         w_pass(4)
+        quant(1)
+        cast(3, "h3", 4.0, 0.0, CW)
+        w_quant(3)
         w_pass(5)
-        w_pass(6)
-        square("y5", "x2", 4.0, -2.5, CB)
-        quant(2)
+        square("y4", "x2", 2.0, -1.0, CB)
         w_pass(7)
         w_load(5)
-        square("y5", "x2", 4.0, -2.5, CA)
+        w_quant(5)
         cast(4, "y4", 2.0, -1.0, CA)
         cast(4, "y4", 2.0, -1.0, CB)
         w_quant(4)
-        w_quant(5)
-        w_quant(6)
+        square("y5", "x2", 4.0, -2.5, CA)
+        quant(2)
+        w_pass(6)
+        square("y5", "x2", 4.0, -2.5, CB)
         w_quant(7)
-        w_pass(8)
-        silu(1)
         silu(3)
+        w_pass(8, (False, True))
         silu(4)
+        silu(1)
         silu(5)
-        w_pass(9)
+        w_quant(6)
+        quant(3)
+        w_pass(9, (False, True))
         silu(0)
         silu(2)
         silu(6)
@@ -413,9 +413,7 @@ def tile_kantlinear_kernel(tc, x, base_weight, cheby_weight, out):
         silu(8)
         square("y6", "h3", 16.0, 0.0, CA)
         square("y6", "h3", 16.0, 0.0, CB)
-        to_g(5, shifted_product("y5", 1.25, "x"), CA)
-        quant(3)
-        to_g(5, shifted_product("y5", 1.25, "x"), CB)
+        to_g(5, shifted_product("y5", 1.25, "x"), CW)
         w_quant(8)
         w_quant(9)
         spline(2, 0, 4)
@@ -431,7 +429,7 @@ def tile_kantlinear_kernel(tc, x, base_weight, cheby_weight, out):
         spline(0, 8, 10)
         spline(1, 8, 10)
         product("t7", "y4", 0.5, "h3", CB)
-        cast(6, "y6", 0.125, -1.0, CA, True)
+        cast(6, "y6", 0.125, -1.0, CA)
         store(0)
         square("y4", "y4", 2.0, -1.0, CA)
         square("y4", "y4", 2.0, -1.0, CB)
@@ -445,32 +443,31 @@ def tile_kantlinear_kernel(tc, x, base_weight, cheby_weight, out):
         cast(6, "y6", 0.125, -1.0, CB, True)
         spline(3, 8, 10)
         quant(4)
-        to_g(7, scaled_minus("t7", 16.0, "x"), CA)
-        to_g(7, scaled_minus("t7", 16.0, "x"), CB)
-        store(2)
-        store(3)
         base(4)
+        to_g(7, scaled_minus("t7", 16.0, "x"), CW)
+        to_g(9, shifted_product("y6", 12.0, "h3"), CW, d_range=(0, 2))
         spline(4)
         quant(5)
+        store(2)
         cast(8, "y4", 2.0, -1.0, CA, True)
         cast(8, "y4", 2.0, -1.0, CB, True)
         base(5)
         store(4)
+        store(3)
         spline(5)
-        to_g(9, shifted_product("y6", 12.0, "h3"), CW, d_range=(4, 8))
         quant(6)
+        to_g(9, shifted_product("y6", 12.0, "h3"), CW, d_range=(4, 8))
         base(6)
         base(7)
         to_g(9, shifted_product("y6", 12.0, "h3"), CW, d_range=(8, 10))
-        to_g(9, shifted_product("y6", 12.0, "h3"), CW, d_range=(0, 2))
         spline(6)
         quant(7, 0, 4)
         spline(7, 0, 4)
-        to_g(9, shifted_product("y6", 12.0, "h3"), CW, d_range=(2, 4))
         quant(7, 4, 8)
         spline(7, 4, 8)
-        store(5)
+        to_g(9, shifted_product("y6", 12.0, "h3"), CW, d_range=(2, 4))
         quant(7, 8, 10)
         spline(7, 8, 10)
         store(6)
+        store(5)
         store(7)

@@ -113,10 +113,9 @@ def tile_kantlinear_kernel(tc, x, base_weight, cheby_weight, out):
 
         def x_transpose(t):
             words = xs[:, t, :].bitcast(F32)
+            col = XROWS * (t % 2)
             for u in range(2):
-                nc.tensor.transpose(
-                    xp[t // 2][:, u, P * (t % 2) : P * (t % 2) + P], words[:, P * u : P * u + P], ident[:]
-                )
+                nc.tensor.transpose(xp[t // 2][:, u, col : col + P], words[:, P * u : P * u + P], ident[:])
 
         def copy_out(on_act, dst, src):
             if on_act:
@@ -124,13 +123,12 @@ def tile_kantlinear_kernel(tc, x, base_weight, cheby_weight, out):
             else:
                 nc.vector.tensor_copy(out=dst, in_=src)
 
-        def x_copy(t, on_act):
-            col = P * (t % 2)
-            if t < 8:
+        def x_copy(k, on_act):
+            if k < 4:
                 copy_out(
                     on_act,
-                    xgw[:, :, 12 * t : 12 * t + 12, :],
-                    xp[t // 2][:, :, col : col + XROWS].rearrange("p u (e d) -> p d e u", e=12, d=ND),
+                    xgw[:, :, 24 * k : 24 * k + 24, :],
+                    xp[k][:, :, 0 : 2 * XROWS].rearrange("p u (e d) -> p d e u", e=24, d=ND),
                 )
             else:
                 copy_out(
@@ -176,17 +174,17 @@ def tile_kantlinear_kernel(tc, x, base_weight, cheby_weight, out):
         scodes = keep.tile([P, B], U32, name="scodes", align_bytes=64)
         sscales = keep.tile([P, B], U8, name="sscales", align_bytes=64)
 
-        def silu(t):
+        def silu(k):
             halves = (
-                xp[t // 2][:]
+                xp[k][:]
                 .rearrange("p u c -> p (u c)")
                 .bitcast(BF16)
                 .rearrange("p (u c e) -> p u c e", u=2, c=256, e=2)
             )
-            c0 = P * (t % 2) if t < 8 else 64
-            n_col = XROWS if t < 8 else 64
+            c0 = 0 if k < 4 else 64
+            n_col = 2 * XROWS if k < 4 else 64
             nc.scalar.activation(
-                out=sg[:, XROWS * t : XROWS * t + n_col, :].rearrange("p c (u e) -> p c u e", u=2),
+                out=sg[:, 2 * XROWS * k : 2 * XROWS * k + n_col, :].rearrange("p c (u e) -> p c u e", u=2),
                 in_=halves[:, :, c0 : c0 + n_col, :].rearrange("p u c e -> p c u e"),
                 func=ACTF.Silu,
             )
@@ -347,21 +345,17 @@ def tile_kantlinear_kernel(tc, x, base_weight, cheby_weight, out):
         x_transpose(1)
         x_transpose(2)
         x_transpose(3)
+        x_transpose(4)
         x_transpose(5)
         x_transpose(6)
         x_transpose(7)
         x_transpose(8)
         x_copy(0, True)
         x_copy(1, True)
-        x_copy(2, True)
-        x_copy(3, True)
-        x_copy(5, False)
-        x_transpose(4)
         square("x2", "x", 1.0, 0.0, CA)
+        x_copy(2, False)
+        x_copy(3, True)
         x_copy(4, True)
-        x_copy(6, True)
-        x_copy(7, True)
-        x_copy(8, True)
         square("x2", "x", 1.0, 0.0, CB)
         to_g(1, plain_copy("x"), CA)
         quant(0)
@@ -376,59 +370,55 @@ def tile_kantlinear_kernel(tc, x, base_weight, cheby_weight, out):
         w_quant(0)
         w_quant(1)
         w_quant(2)
-        w_load(4)
+        w_load(3)
         cast(2, "x2", 2.0, -1.0, CB)
         w_pass(3)
-        w_load(3)
+        w_load(4)
         w_pass(4)
         quant(1)
         cast(3, "h3", 4.0, 0.0, CW)
         w_quant(3)
         w_pass(5)
         square("y4", "x2", 2.0, -1.0, CB)
-        w_pass(7)
+        w_pass(6)
         w_load(5)
-        w_quant(5)
+        w_quant(4)
         cast(4, "y4", 2.0, -1.0, CA)
         cast(4, "y4", 2.0, -1.0, CB)
-        w_quant(4)
+        w_quant(5)
         square("y5", "x2", 4.0, -2.5, CA)
         quant(2)
-        w_pass(6)
+        w_pass(7)
         square("y5", "x2", 4.0, -2.5, CB)
-        w_quant(7)
-        silu(3)
-        w_pass(8, (False, True))
-        silu(4)
-        silu(1)
-        silu(5)
         w_quant(6)
+        w_pass(8, (False, True))
+        silu(0)
+        silu(1)
+        w_quant(7)
         quant(3)
         w_pass(9, (False, True))
-        silu(0)
         silu(2)
-        silu(6)
         w_pass(10)
-        silu(7)
-        silu(8)
+        silu(3)
+        silu(4)
         square("y6", "h3", 16.0, 0.0, CA)
         square("y6", "h3", 16.0, 0.0, CB)
         to_g(5, shifted_product("y5", 1.25, "x"), CW)
         w_quant(8)
         w_quant(9)
-        spline(2, 0, 4)
         w_quant(10)
         spline(0, 0, 4)
         silu_quant()
         spline(0, 4, 8)
         product("t7", "y4", 0.5, "h3", CA)
-        base(1)
         base(0)
+        base(1)
         spline(1, 0, 4)
         spline(1, 4, 8)
         spline(0, 8, 10)
         spline(1, 8, 10)
         product("t7", "y4", 0.5, "h3", CB)
+        spline(2, 0, 4)
         cast(6, "y6", 0.125, -1.0, CA)
         store(0)
         square("y4", "y4", 2.0, -1.0, CA)
@@ -452,8 +442,8 @@ def tile_kantlinear_kernel(tc, x, base_weight, cheby_weight, out):
         cast(8, "y4", 2.0, -1.0, CA, True)
         cast(8, "y4", 2.0, -1.0, CB, True)
         base(5)
-        store(4)
         store(3)
+        store(4)
         spline(5)
         quant(6)
         to_g(9, shifted_product("y6", 12.0, "h3"), CW, d_range=(4, 8))
@@ -468,6 +458,6 @@ def tile_kantlinear_kernel(tc, x, base_weight, cheby_weight, out):
         to_g(9, shifted_product("y6", 12.0, "h3"), CW, d_range=(2, 4))
         quant(7, 8, 10)
         spline(7, 8, 10)
-        store(6)
         store(5)
+        store(6)
         store(7)

@@ -24,7 +24,7 @@ XROWS = 120
 CA = (0, 48)
 CB = (48, EP)
 CW = (0, EP)
-MANUAL = True
+MANUAL = False
 
 
 def count_e(d):
@@ -284,12 +284,12 @@ def tile_kantlinear_kernel(tc, x, base_weight, cheby_weight, out):
                 op1=ALU.mult,
             )
 
-        def to_g(n, emit, chunk, emit_act=None, d_range=(0, ND)):
+        def to_g(n, emit, chunk, emit_act=None, d_range=(0, ND), vector_below=False):
             for d0, d1, e0, e1, j, c0, m0, first, last in runs(n, d_range[0], d_range[1], chunk[0], chunk[1]):
                 g = g_tile(j)
                 parts = [(e0, e1, False)]
                 if emit_act is not None:
-                    lo = e0 + (-m0) % 4 if first else e0
+                    lo = e0 + (-m0) % 4 if first or (vector_below and e0 == chunk[0]) else e0
                     hi = e1 - (m0 + e1 - e0) % 4 if last else e1
                     if lo < hi:
                         parts = [(lo, hi, True), (e0, lo, False), (hi, e1, False)]
@@ -313,8 +313,14 @@ def tile_kantlinear_kernel(tc, x, base_weight, cheby_weight, out):
 
             return on_scalar
 
-        def cast(n, src, scale, bias, chunk, on_act=False):
-            to_g(n, affine(src, scale, bias), chunk, affine_act(src, scale, bias) if on_act else None)
+        def cast(n, src, scale, bias, chunk, on_act=False, vector_below=False):
+            to_g(
+                n,
+                affine(src, scale, bias),
+                chunk,
+                affine_act(src, scale, bias) if on_act else None,
+                vector_below=vector_below,
+            )
 
         def shifted_product(a, shift, b):
             def on_vector(dst, where):
@@ -430,7 +436,7 @@ def tile_kantlinear_kernel(tc, x, base_weight, cheby_weight, out):
         spline(3, 0, 4)
         spline(2, 8, 10)
         spline(3, 4, 8)
-        cast(6, "y6", 0.125, -1.0, CB, True)
+        cast(6, "y6", 0.125, -1.0, CB, True, True)
         spline(3, 8, 10)
         quant(4)
         base(4)

@@ -24,7 +24,7 @@ XROWS = 120
 CA = (0, 48)
 CB = (48, EP)
 CW = (0, EP)
-MANUAL = False
+MANUAL = True
 
 
 def count_e(d):

from contextlib import ExitStack

import concourse.mybir as mybir
from concourse.masks import make_identity

F32 = mybir.dt.float32
BF16 = mybir.dt.bfloat16
U32 = mybir.dt.uint32
U8 = mybir.dt.uint8
FP8X4 = mybir.dt.float8_e4m3fn_x4
ALU = mybir.AluOpType
ACTF = mybir.ActivationFunctionType

P = 128
B = 1024
IN = 512
OUT = 512
ORDER = 10
FLOPS = 2 * B * OUT * (IN + IN * ORDER)

ND = 10
EP = 104
XROWS = 120
CA = (0, 48)
CB = (48, EP)
CW = (0, EP)
MANUAL = True


def count_e(d):
    return 103 if d < 4 else 102


def runs(n, da, db, ea, eb):
    found = []
    d0 = da
    while d0 < db:
        q = (4 * n + d0) // 10
        d1 = d0
        while d1 < db and (4 * n + d1) // 10 == q and count_e(d1) == count_e(d0):
            d1 += 1
        start = 102 * n + q
        lo = ea
        hi = min(eb, count_e(d0))
        while lo < hi:
            j = (start + lo) // P
            end = min(hi, P * (j + 1) - start)
            found.append((d0, d1, lo, end, j, (4 * n + d0) % 10, (start + lo) % P, lo == 0, end == count_e(d0)))
            lo = end
        d0 = d1
    return found


def tile_kantlinear_kernel(tc, x, base_weight, cheby_weight, out):
    nc = tc.nc
    with ExitStack() as ctx:
        if MANUAL:
            ctx.enter_context(tc.manual_schedule())
        keep = ctx.enter_context(tc.tile_pool(name="keep", bufs=1))
        wraw = ctx.enter_context(tc.tile_pool(name="wraw", bufs=3))
        wgrp = ctx.enter_context(tc.tile_pool(name="wgrp", bufs=3))
        gpool = ctx.enter_context(tc.tile_pool(name="gpool", bufs=3))
        cpool = ctx.enter_context(tc.tile_pool(name="cpool", bufs=4))
        opool = ctx.enter_context(tc.tile_pool(name="opool", bufs=3))
        psum = ctx.enter_context(tc.psum_pool(name="psum", bufs=1))

        def bank(i, name):
            return psum.tile([P, 2, 256], F32, tag="bank%d" % i, name=name)

        warm = keep.tile([P, 1], F32, name="warm")
        nc.vector.memset(warm[:], 0.0)
        nc.scalar.activation(out=warm[:], in_=warm[:], func=ACTF.Silu)

        xs = keep.tile([P, 9, IN], BF16, name="xs")
        for t in range(9):
            r0 = XROWS * t if t < 8 else B - P
            nc.sync.dma_start(out=xs[:, t, :], in_=x[r0 : r0 + P, :])
        wv = cheby_weight.rearrange("o i k -> o (i k)").rearrange("(t p) k -> p t k", p=P)
        bv = base_weight.rearrange("(t p) k -> p t k", p=P)
        raws = {}

        def w_load(cc):
            if cc < 5:
                raws[cc] = wraw.tile([P, 4, 1024], BF16, tag="wr", name="wr%d" % cc)
                nc.sync.dma_start(out=raws[cc][:], in_=wv[:, :, 1024 * cc : 1024 * cc + 1024])
            else:
                raws[cc] = wraw.tile([P, 4, IN], BF16, tag="wr", name="wrb")
                nc.sync.dma_start(out=raws[cc][:], in_=bv)

        ident = keep.tile([P, P], F32, name="ident")
        make_identity(nc, ident[:])

        xg = keep.tile([P, ND, EP, 4], BF16, name="xg", align_bytes=64)
        nc.vector.memset(xg[:, :, 100:EP, :], 0.0)
        xgw = (
            xg[:]
            .rearrange("p d e t -> p (d e t)")
            .bitcast(F32)
            .rearrange("p (d e u) -> p d e u", d=ND, e=EP, u=2)
        )

        gt = {}

        def g_tile(j):
            if j not in gt:
                gt[j] = gpool.tile([P, ORDER, P, 4], BF16, tag="G", name="G%d" % j, align_bytes=64)
            return gt[j]

        for d0, d1, e0, e1, j, c0, m0, first, last in runs(0, 0, ND, 0, EP):
            nc.vector.memset(g_tile(j)[:, c0 : c0 + d1 - d0, m0 : m0 + e1 - e0, :], 1.0)

        xp = [bank(k, "xp%d" % k) for k in range(5)]

        def x_transpose(t):
            words = xs[:, t, :].bitcast(F32)
            col = XROWS * (t % 2)
            for u in range(2):
                nc.tensor.transpose(xp[t // 2][:, u, col : col + P], words[:, P * u : P * u + P], ident[:])

        def copy_out(on_act, dst, src):
            if on_act:
                nc.scalar.copy(out=dst, in_=src)
            else:
                nc.vector.tensor_copy(out=dst, in_=src)

        def x_copy(k, on_act):
            if k < 4:
                copy_out(
                    on_act,
                    xgw[:, :, 24 * k : 24 * k + 24, :],
                    xp[k][:, :, 0 : 2 * XROWS].rearrange("p u (e d) -> p d e u", e=24, d=ND),
                )
            else:
                copy_out(
                    on_act,
                    xgw[:, :, 96:102, :],
                    xp[4][:, :, 64:124].rearrange("p u (e d) -> p d e u", e=6, d=ND),
                )
                copy_out(on_act, xgw[:, 0:4, 102, :], xp[4][:, :, 124:128].rearrange("p u d -> p d u"))

        wcodes = keep.tile([P, ORDER + 1, OUT], U32, name="wcodes", align_bytes=64)
        wscales = keep.tile([P, ORDER + 1, OUT], U8, name="wscales", align_bytes=64)
        state = {"wbank": 0}
        grouped = {}

        def w_quant(g):
            nc.vector.quantize_mx(
                out=wcodes[:, g, :].bitcast(FP8X4),
                scales=wscales[:, g, :],
                in_=grouped[g][:].rearrange("p o t -> p (o t)"),
            )

        def w_pass(g, act_halves=(True, True)):
            raw = raws[g // 2]
            word0 = 256 * (g % 2)
            grouped[g] = wgrp.tile([P, OUT, 4], BF16, tag="wg", name="wg%d" % g, align_bytes=64)
            gw = grouped[g][:].rearrange("p o t -> p (o t)").bitcast(F32).rearrange("p (o u) -> p o u", u=2)
            for half in range(2):
                wt = bank(5 + state["wbank"] % 3, "wt%d_%d" % (g, half))
                state["wbank"] += 1
                for u in range(2):
                    for oo in range(2):
                        words = raw[:, 2 * half + oo, :].bitcast(F32)
                        nc.tensor.transpose(
                            wt[:, u, P * oo : P * oo + P],
                            words[:, word0 + P * u : word0 + P * u + P],
                            ident[:],
                        )
                copy_out(
                    act_halves[half], gw[:, 256 * half : 256 * half + 256, :], wt[:].rearrange("p u o -> p o u")
                )

        sg = keep.tile([P, B, 4], BF16, name="sg", align_bytes=64)
        scodes = keep.tile([P, B], U32, name="scodes", align_bytes=64)
        sscales = keep.tile([P, B], U8, name="sscales", align_bytes=64)

        def silu(k):
            halves = (
                xp[k][:]
                .rearrange("p u c -> p (u c)")
                .bitcast(BF16)
                .rearrange("p (u c e) -> p u c e", u=2, c=256, e=2)
            )
            c0 = 0 if k < 4 else 64
            n_col = 2 * XROWS if k < 4 else 64
            nc.scalar.activation(
                out=sg[:, 2 * XROWS * k : 2 * XROWS * k + n_col, :].rearrange("p c (u e) -> p c u e", u=2),
                in_=halves[:, :, c0 : c0 + n_col, :].rearrange("p u c e -> p c u e"),
                func=ACTF.Silu,
            )

        def silu_quant():
            nc.vector.quantize_mx(
                out=scodes[:].bitcast(FP8X4), scales=sscales[:], in_=sg[:].rearrange("p c t -> p (c t)")
            )

        codes = {}
        sums = {}

        def quant(j, c0=0, c1=ORDER):
            if j not in codes:
                codes[j] = (
                    cpool.tile([P, ORDER * P], U32, tag="fc", name="fc%d" % j, align_bytes=64),
                    cpool.tile([P, ORDER * P], U8, tag="fs", name="fs%d" % j, align_bytes=64),
                )
            fc, fs = codes[j]
            flat = gt[j][:].rearrange("p c m t -> p (c m t)")
            while c0 < c1:
                width = 8 if c1 - c0 >= 8 else 4 if c1 - c0 >= 4 else 2 if c1 - c0 >= 2 else 1
                nc.vector.quantize_mx(
                    out=fc[:, P * c0 : P * (c0 + width)].bitcast(FP8X4),
                    scales=fs[:, P * c0 : P * (c0 + width)],
                    in_=flat[:, 4 * P * c0 : 4 * P * (c0 + width)],
                )
                c0 += width

        def base(j):
            accb = psum.tile([P, OUT], F32, tag="bank%d" % (4 + j % 4), name="accb%d" % j)
            nc.tensor.matmul_mx(
                out=accb[:],
                lhsT=scodes[:, P * j : P * j + P].bitcast(FP8X4),
                lhsT_scale=sscales[:, P * j : P * j + P],
                rhs=wcodes[:, ORDER, :].bitcast(FP8X4),
                rhs_scale=wscales[:, ORDER, :],
                start=True,
                stop=True,
            )
            bsb = opool.tile([P, OUT], F32, tag="bsb", name="bsb%d" % j)
            nc.scalar.copy(out=bsb[:], in_=accb[:])
            sums[j] = [sums[j][0] if j in sums else None, bsb]

        def spline(j, c0=0, c1=ORDER):
            fc, fs = codes[j]
            if c0 == 0:
                sums[j] = [
                    psum.tile([P, OUT], F32, tag="bank%d" % (j % 4), name="accs%d" % j),
                    sums[j][1] if j in sums else None,
                ]
            for c in range(c0, c1):
                nc.tensor.matmul_mx(
                    out=sums[j][0][:],
                    lhsT=fc[:, P * c : P * c + P].bitcast(FP8X4),
                    lhsT_scale=fs[:, P * c : P * c + P],
                    rhs=wcodes[:, c, :].bitcast(FP8X4),
                    rhs_scale=wscales[:, c, :],
                    start=(c == 0),
                    stop=(c == ORDER - 1),
                )

        def store(j):
            accs, bsb = sums[j]
            osb = opool.tile([P, OUT], F32, tag="osb", name="osb%d" % j)
            nc.vector.scalar_tensor_tensor(
                out=osb[:], in0=accs[:], scalar=0.1, in1=bsb[:], op0=ALU.mult, op1=ALU.add
            )
            nc.sync.dma_start(out=out[P * j : P * j + P, :], in_=osb[:])

        tags = {"x2": "ta", "y6": "ta", "h3": "tb", "y4": "tc", "y5": "td", "t7": "td"}
        temps = {"x": xg}

        def tmp(name):
            if name not in temps:
                temps[name] = keep.tile([P, ND, EP, 4], F32, tag=tags[name], name=name)
            return temps[name]

        def square(dst, src, scale, bias, chunk):
            e0, e1 = chunk
            nc.scalar.activation(
                out=tmp(dst)[:, :, e0:e1, :],
                in_=tmp(src)[:, :, e0:e1, :],
                func=ACTF.Square,
                scale=scale,
                bias=bias,
            )

        def product(dst, a, shift, b, chunk):
            e0, e1 = chunk
            nc.vector.scalar_tensor_tensor(
                out=tmp(dst)[:, :, e0:e1, :],
                in0=tmp(a)[:, :, e0:e1, :],
                scalar=shift,
                in1=tmp(b)[:, :, e0:e1, :],
                op0=ALU.subtract,
                op1=ALU.mult,
            )

        def to_g(n, emit, chunk, emit_act=None, d_range=(0, ND), vector_below=False):
            for d0, d1, e0, e1, j, c0, m0, first, last in runs(n, d_range[0], d_range[1], chunk[0], chunk[1]):
                g = g_tile(j)
                parts = [(e0, e1, False)]
                if emit_act is not None:
                    lo = e0 + (-m0) % 4 if first or (vector_below and e0 == chunk[0]) else e0
                    hi = e1 - (m0 + e1 - e0) % 4 if last else e1
                    if lo < hi:
                        parts = [(lo, hi, True), (e0, lo, False), (hi, e1, False)]
                for a, b, on_act in parts:
                    if a == b:
                        continue
                    dst = g[:, c0 : c0 + d1 - d0, m0 + a - e0 : m0 + b - e0, :]
                    (emit_act if on_act else emit)(dst, (slice(None), slice(d0, d1), slice(a, b), slice(None)))

        def affine(src, scale, bias):
            def on_vector(dst, where):
                nc.vector.tensor_scalar(
                    out=dst, in0=tmp(src)[where], scalar1=scale, scalar2=bias, op0=ALU.mult, op1=ALU.add
                )

            return on_vector

        def affine_act(src, scale, bias):
            def on_scalar(dst, where):
                nc.scalar.activation(out=dst, in_=tmp(src)[where], func=ACTF.Identity, scale=scale, bias=bias)

            return on_scalar

        def cast(n, src, scale, bias, chunk, on_act=False, vector_below=False):
            to_g(
                n,
                affine(src, scale, bias),
                chunk,
                affine_act(src, scale, bias) if on_act else None,
                vector_below=vector_below,
            )

        def shifted_product(a, shift, b):
            def on_vector(dst, where):
                nc.vector.scalar_tensor_tensor(
                    out=dst, in0=tmp(a)[where], scalar=shift, in1=tmp(b)[where], op0=ALU.subtract, op1=ALU.mult
                )

            return on_vector

        def scaled_minus(a, scale, b):
            def on_vector(dst, where):
                nc.vector.scalar_tensor_tensor(
                    out=dst, in0=tmp(a)[where], scalar=scale, in1=tmp(b)[where], op0=ALU.mult, op1=ALU.subtract
                )

            return on_vector

        def plain_copy(src):
            def on_vector(dst, where):
                nc.vector.tensor_copy(out=dst, in_=tmp(src)[where])

            return on_vector

        w_load(0)
        w_load(1)
        w_load(2)
        x_transpose(0)
        x_transpose(1)
        x_transpose(2)
        x_transpose(3)
        x_transpose(4)
        x_transpose(5)
        x_transpose(6)
        x_transpose(7)
        x_transpose(8)
        x_copy(0, True)
        x_copy(1, True)
        square("x2", "x", 1.0, 0.0, CA)
        x_copy(2, False)
        x_copy(3, True)
        x_copy(4, True)
        square("x2", "x", 1.0, 0.0, CB)
        to_g(1, plain_copy("x"), CA)
        quant(0)
        cast(2, "x2", 2.0, -1.0, CA)
        product("h3", "x2", 0.75, "x", CA)
        w_pass(0)
        to_g(1, plain_copy("x"), CB)
        w_pass(1)
        w_pass(2)
        product("h3", "x2", 0.75, "x", CB)
        square("y4", "x2", 2.0, -1.0, CA)
        w_quant(0)
        w_quant(1)
        w_quant(2)
        w_load(3)
        cast(2, "x2", 2.0, -1.0, CB)
        w_pass(3)
        w_load(4)
        w_pass(4)
        quant(1)
        cast(3, "h3", 4.0, 0.0, CW)
        w_quant(3)
        w_pass(5)
        square("y4", "x2", 2.0, -1.0, CB)
        w_pass(6)
        w_load(5)
        w_quant(4)
        cast(4, "y4", 2.0, -1.0, CA)
        cast(4, "y4", 2.0, -1.0, CB)
        w_quant(5)
        square("y5", "x2", 4.0, -2.5, CA)
        quant(2)
        w_pass(7)
        square("y5", "x2", 4.0, -2.5, CB)
        w_quant(6)
        w_pass(8, (False, True))
        silu(0)
        silu(1)
        w_quant(7)
        quant(3)
        w_pass(9, (False, True))
        silu(2)
        w_pass(10)
        silu(3)
        silu(4)
        square("y6", "h3", 16.0, 0.0, CA)
        square("y6", "h3", 16.0, 0.0, CB)
        to_g(5, shifted_product("y5", 1.25, "x"), CW)
        w_quant(8)
        w_quant(9)
        w_quant(10)
        spline(0, 0, 4)
        silu_quant()
        spline(0, 4, 8)
        product("t7", "y4", 0.5, "h3", CA)
        base(0)
        base(1)
        spline(1, 0, 4)
        spline(1, 4, 8)
        spline(0, 8, 10)
        spline(1, 8, 10)
        product("t7", "y4", 0.5, "h3", CB)
        spline(2, 0, 4)
        cast(6, "y6", 0.125, -1.0, CA)
        store(0)
        square("y4", "y4", 2.0, -1.0, CA)
        square("y4", "y4", 2.0, -1.0, CB)
        store(1)
        spline(2, 4, 8)
        base(2)
        base(3)
        spline(3, 0, 4)
        spline(2, 8, 10)
        spline(3, 4, 8)
        cast(6, "y6", 0.125, -1.0, CB, True, True)
        spline(3, 8, 10)
        quant(4)
        base(4)
        to_g(7, scaled_minus("t7", 16.0, "x"), CW)
        to_g(9, shifted_product("y6", 12.0, "h3"), CW, d_range=(0, 2))
        spline(4)
        quant(5)
        store(2)
        cast(8, "y4", 2.0, -1.0, CA, True)
        cast(8, "y4", 2.0, -1.0, CB, True)
        base(5)
        store(3)
        store(4)
        spline(5)
        quant(6)
        to_g(9, shifted_product("y6", 12.0, "h3"), CW, d_range=(4, 8))
        base(6)
        base(7)
        to_g(9, shifted_product("y6", 12.0, "h3"), CW, d_range=(8, 10))
        spline(6)
        quant(7, 0, 4)
        spline(7, 0, 4)
        quant(7, 4, 8)
        spline(7, 4, 8)
        to_g(9, shifted_product("y6", 12.0, "h3"), CW, d_range=(2, 4))
        quant(7, 8, 10)
        spline(7, 8, 10)
        store(5)
        store(6)
        store(7)
